import numpy as np
import ml_dtypes


def mxq(x, axis, fmt="e4m3"):
    dtype, down = {"e4m3": (ml_dtypes.float8_e4m3fn, 7), "e5m2": (ml_dtypes.float8_e5m2, 14)}[fmt]
    v = np.moveaxis(np.asarray(x, np.float32).astype(ml_dtypes.bfloat16).astype(np.float64), axis, -1)
    blocks = v.reshape(v.shape[:-1] + (-1, 32))
    amax = np.abs(blocks).max(-1, keepdims=True)
    byte = np.maximum(np.where(amax > 0, np.frexp(amax)[1] - 1 + 127, 0) - down, 1)
    scale = np.exp2(byte - 127.0)
    codes = (blocks / scale).astype(np.float32).astype(dtype).astype(np.float64)
    return np.moveaxis((codes * scale).reshape(v.shape), -1, axis)


WIDE = False


def mx_kscale(k):
    if not WIDE:
        return np.ones(k)
    levels = np.array([10, -10, 5, -5, 0])
    a = np.random.permutation(np.resize(levels, k // 512 * 4)).reshape(k // 512, 4)
    idx = np.arange(k)
    return np.exp2(a[idx // 512, idx % 128 // 32])


BF16 = ml_dtypes.bfloat16


def bf(x):
    return np.asarray(x, np.float32).astype(BF16)


def f64(x):
    return np.asarray(x).astype(np.float64)


E2M1 = np.array([0.0, 0.5, 1.0, 1.5, 2.0, 3.0, 4.0, 6.0, -0.0, -0.5, -1.0, -1.5, -2.0, -3.0, -4.0, -6.0])


def pack_weight(w, fmt):
    k, n = w.shape
    w = f64(bf(w)).reshape(k // 32, 32, n)
    amax = np.abs(w).max(1)
    if fmt == "e4m3":
        byte = np.frexp(amax)[1] - 1 + 127 - 7
    else:
        mant, ex = np.frexp(amax / 6.0)
        byte = np.where(mant > 0.5, ex, ex - 1) + 127
    byte = np.clip(np.where(amax > 0, byte, 1), 1, 254)
    scaled = (w * np.exp2(127.0 - byte)[:, None, :]).reshape(k, n).astype(np.float32)
    by_word = np.ascontiguousarray(scaled.reshape(k // 512, 128, 4, n).transpose(0, 1, 3, 2))
    if fmt == "e4m3":
        words = by_word.astype(ml_dtypes.float8_e4m3fn).view(np.uint8)
    else:
        c = by_word.astype(ml_dtypes.float4_e2m1fn).view(np.uint8) & 0xF
        words = c[..., 0::2] | (c[..., 1::2] << 4)
    return np.ascontiguousarray(words), np.ascontiguousarray(byte.astype(np.uint8).reshape(k // 512, 16, n))


def unpack_weight(words, scales, fmt):
    g, p, n, _ = words.shape
    if fmt == "e4m3":
        vals = np.ascontiguousarray(words).view(ml_dtypes.float8_e4m3fn).astype(np.float64)
    else:
        nib = np.empty((g, p, n, 4), np.uint8)
        nib[..., 0::2] = words & 0xF
        nib[..., 1::2] = words >> 4
        vals = E2M1[nib]
    vals = vals * np.repeat(np.exp2(scales.astype(np.float64) - 127.0), 8, axis=1)[..., None]
    return vals.transpose(0, 1, 3, 2).reshape(g * 512, n)


B, T, C, CO, HS, DW, DA, DV, DG = 4, 128, 16384, 512, 64, 128, 128, 128, 256


def sigmoid(u):
    return 1.0 / (1.0 + np.exp(-u))


def setup_inputs():
    n = np.random.standard_normal
    s = mx_kscale(C)
    x = bf(n((B, T, C)) * s)
    x_v = bf(n((1, 1, C)) * 0.3)
    W_v_words, W_v_scales = pack_weight((n((CO, C)) / np.sqrt(C) / s).T, "e4m3")
    return {
        "x": x,
        "x_v": x_v,
        "W_v_words": W_v_words,
        "W_v_scales": W_v_scales,
        "v_hid": bf(n((B, T, DV))),
        "v2": bf(n((DV, CO)) / np.sqrt(DV)),
        "v0": bf(0.73 + n((1, 1, CO)) * 0.2),
        "v_first": bf(n((B, T, CO))),
    }


def reference(x, x_v, W_v_words, W_v_scales, v_hid, v2, v0, v_first):
    x = f64(x)
    prev = np.concatenate([np.zeros_like(x[:, :1]), x[:, :-1]], axis=1)
    xv = x + (prev - x) * f64(x_v)
    v = mxq(xv, 2, "e4m3") @ unpack_weight(W_v_words, W_v_scales, "e4m3")
    mix = sigmoid(f64(v0) + f64(v_hid) @ f64(v2))
    return v + (f64(v_first) - v) * mix

@@ -1,0 +1,242 @@
+from contextlib import ExitStack
+
+import concourse.mybir as mybir
+from concourse.masks import make_identity
+
+F32 = mybir.dt.float32
+BF16 = mybir.dt.bfloat16
+U8 = mybir.dt.uint8
+U32 = mybir.dt.uint32
+I32 = mybir.dt.int32
+FP8X4 = mybir.dt.float8_e4m3fn_x4
+ACT = mybir.ActivationFunctionType
+ALU = mybir.AluOpType
+
+P = 128
+SEQS = 4
+TOKENS = SEQS * P
+CHANNELS = 16384
+CO = 512
+DV = 128
+PACK = 4
+K_PASS = P * PACK
+GROUPS = CHANNELS // K_PASS
+HALVES = 2
+WORDS = K_PASS // 2
+
+PLANES = 4
+QUADRANTS = 4
+
+LOAD_AHEAD = 6
+X_BUFS = LOAD_AHEAD + 2
+W_BUFS = LOAD_AHEAD + 4
+CARRY_TILES = 2 * PACK
+RUN = 4
+SCALAR_TOKENS = 256
+
+FLOPS = 2 * TOKENS * CHANNELS * CO + 2 * TOKENS * DV * CO
+
+
+def tile_full_tmix_params_pb_k_kernel(
+    tc, x, x_v, W_v_words, W_v_scales, v_hid, v2, v0, v_first, out
+):
+    nc = tc.nc
+    with ExitStack() as ctx:
+        const = ctx.enter_context(tc.tile_pool(name="const", bufs=1))
+        x_pool = ctx.enter_context(tc.tile_pool(name="x_pool", bufs=X_BUFS))
+        w_pool = ctx.enter_context(tc.tile_pool(name="w_pool", bufs=W_BUFS))
+        work = ctx.enter_context(tc.tile_pool(name="work", bufs=3))
+        psum_t = ctx.enter_context(tc.psum_pool(name="psum_t", bufs=4))
+        psum_acc = ctx.enter_context(tc.psum_pool(name="psum_acc", bufs=1))
+        ctx.enter_context(tc.manual_schedule())
+
+        w_planes = const.tile([P, GROUPS // PLANES, CO], U8, name="w_planes", align_bytes=64)
+        nc.vector.memset(w_planes[:].bitcast(I32), 0)
+        x_tiles = {}
+        w_tiles = {}
+
+        def load_group(g):
+            x_g = x_pool.tile([P, SEQS, K_PASS], BF16, name="x_g")
+            nc.sync.dma_start(
+                out=x_g[:],
+                in_=x[:, :, K_PASS * g : K_PASS * (g + 1)].rearrange("b n k -> n b k"),
+            )
+            x_tiles[g] = x_g
+            if g % PLANES == 0:
+                for q in range(QUADRANTS):
+                    nc.sync.dma_start(
+                        out=w_planes[32 * q : 32 * q + 4 * PLANES, g // PLANES, :].bitcast(I32),
+                        in_=W_v_scales[g : g + PLANES, 4 * q : 4 * q + 4, :].bitcast(I32),
+                    )
+            w_g = w_pool.tile([P, CO], U32, name="w_g", align_bytes=64)
+            nc.sync.dma_start(
+                out=w_g[:].bitcast(I32),
+                in_=W_v_words[g].rearrange("p n t -> p (n t)").bitcast(I32),
+            )
+            w_tiles[g] = w_g
+
+        xv_rows = const.tile([P, K_PASS], BF16, name="xv_rows")
+        nc.vector.memset(xv_rows[:], 0.0)
+        nc.scalar.dma_start(
+            out=xv_rows[0:GROUPS, :], in_=x_v.rearrange("a b (g k) -> (a b g) k", k=K_PASS)
+        )
+        vh = const.tile([P, SEQS, DV], BF16, name="vh")
+        nc.scalar.dma_start(out=vh[:], in_=v_hid.rearrange("b n d -> n b d"))
+        v2_sb = const.tile([DV, CO], BF16, name="v2_sb")
+        nc.scalar.dma_start(out=v2_sb[:], in_=v2)
+        bias_rows = const.tile([P, CO], BF16, name="bias_rows")
+        nc.gpsimd.memset(bias_rows[:], 0.0)
+        nc.scalar.dma_start(out=bias_rows[0:1, :], in_=v0.rearrange("a b c -> (a b) c"))
+        for g in range(LOAD_AHEAD):
+            load_group(g)
+        vf = const.tile([P, SEQS, CO], BF16, name="vf")
+        nc.scalar.dma_start(out=vf[:], in_=v_first.rearrange("b n c -> n b c"))
+
+        ident_f = const.tile([P, P], F32, name="ident_f")
+        make_identity(nc, ident_f[:])
+        ident_b = const.tile([P, P], BF16, name="ident_b")
+        make_identity(nc, ident_b[:])
+        ones = const.tile([P, P], BF16, name="ones")
+        nc.gpsimd.memset(ones[:], 1.0)
+        carry_tiles = []
+        for i in range(CARRY_TILES):
+            carried = const.tile([P, SEQS, P], F32, name="carried%d" % i)
+            nc.vector.memset(carried[:], 0.0)
+            carry_tiles.append(carried)
+
+        xv_ps = psum_t.tile([P, HALVES, P], F32, name="xv_ps", tag="bank")
+        for u in range(HALVES):
+            nc.tensor.transpose(
+                xv_ps[:, u, :], xv_rows[:].bitcast(F32)[:, u:WORDS:HALVES], ident_f[:]
+            )
+        mix_k = const.tile([P, GROUPS, PACK], F32, name="mix_k")
+        nc.vector.tensor_copy(
+            out=mix_k[:].rearrange("p g (u e) -> p u g e", u=HALVES),
+            in_=xv_ps[:].bitcast(BF16).rearrange("p u (g e) -> p u g e", e=2)[:, :, 0:GROUPS, :],
+        )
+        keep_k = const.tile([P, GROUPS, PACK], F32, name="keep_k")
+        nc.vector.tensor_scalar(
+            out=keep_k[:], in0=mix_k[:], scalar1=-1.0, scalar2=1.0, op0=ALU.mult, op1=ALU.add
+        )
+
+        vhT_ps = psum_t.tile([P, SEQS, P], BF16, name="vhT_ps", tag="bank")
+        for b in range(SEQS):
+            nc.tensor.transpose(vhT_ps[:, b, :], vh[:, b, :], ident_b[:])
+        vhT = const.tile([DV, SEQS, P], BF16, name="vhT")
+        nc.vector.tensor_copy(out=vhT[:], in_=vhT_ps[:])
+        gate = const.tile([P, SEQS, CO], F32, name="gate")
+        keep_v = const.tile([P, SEQS, CO], F32, name="keep_v")
+        first_part = const.tile([P, SEQS, CO], F32, name="first_part")
+        for b in range(SEQS):
+            z = psum_acc.tile([P, CO], F32, name="z%d" % b, tag="acc%d" % b)
+            nc.tensor.matmul(out=z[:], lhsT=vhT[:, b, :], rhs=v2_sb[:], start=True, stop=False)
+            nc.tensor.matmul(out=z[:], lhsT=ones[:], rhs=bias_rows[:], start=False, stop=True)
+            nc.scalar.activation(out=gate[:, b, :], in_=z[:], func=ACT.Sigmoid)
+            nc.gpsimd.tensor_scalar(
+                out=keep_v[:, b, :], in0=gate[:, b, :],
+                scalar1=-1.0, scalar2=1.0, op0=ALU.mult, op1=ALU.add,
+            )
+            nc.gpsimd.tensor_tensor(
+                out=first_part[:, b, :], in0=vf[:, b, :], in1=gate[:, b, :], op=ALU.mult
+            )
+        acc = [
+            psum_acc.tile([P, CO], F32, name="acc%d" % b, tag="acc%d" % b) for b in range(SEQS)
+        ]
+
+        banks = {}
+        mixed_tiles = {}
+        grouped_tiles = {}
+
+        def transpose_group(g):
+            words = x_tiles[g][:].bitcast(F32)
+            for u in range(HALVES):
+                bank = psum_t.tile([P, TOKENS], F32, name="bank", tag="bank")
+                for b in range(SEQS):
+                    nc.tensor.transpose(
+                        bank[:, P * b : P * (b + 1)], words[:, b, u:WORDS:HALVES], ident_f[:]
+                    )
+                banks[g, u] = bank
+
+        def shift_and_mix(g):
+            mixed = work.tile([P, PACK, TOKENS], BF16, name="mixed")
+            for u in range(HALVES):
+                by_seq = banks[g, u][:].bitcast(BF16).rearrange(
+                    "p (b n e) -> p b n e", b=SEQS, e=2
+                )
+                for e in range(2):
+                    t = HALVES * u + e
+                    nc.scalar.activation(
+                        out=carry_tiles[(PACK * g + t) % CARRY_TILES][:, :, 1:P],
+                        in_=by_seq[:, :, 0 : P - 1, e],
+                        func=ACT.Copy,
+                        scale=mix_k[:, g, t : t + 1],
+                    )
+            for u in range(HALVES):
+                flat = banks[g, u][:].bitcast(BF16).rearrange("p (n e) -> p n e", e=2)
+                for e in (1, 0):
+                    t = HALVES * u + e
+                    nc.vector.scalar_tensor_tensor(
+                        out=mixed[:, t, :],
+                        in0=flat[:, :, e],
+                        scalar=keep_k[:, g, t : t + 1],
+                        in1=carry_tiles[(PACK * g + t) % CARRY_TILES][:].rearrange(
+                            "p b n -> p (b n)"
+                        ),
+                        op0=ALU.mult,
+                        op1=ALU.add,
+                    )
+            mixed_tiles[g] = mixed
+
+        def regroup(g):
+            grouped = work.tile([P, TOKENS, PACK], BF16, name="grouped", align_bytes=64)
+            src = mixed_tiles[g][:].rearrange("p t (c i) -> p c t i", i=RUN)
+            dst = grouped[:].rearrange("p (c i) t -> p c t i", i=RUN)
+            cut = SCALAR_TOKENS // RUN
+            nc.scalar.copy(out=dst[:, 0:cut], in_=src[:, 0:cut])
+            nc.vector.tensor_copy(out=dst[:, cut:], in_=src[:, cut:])
+            grouped_tiles[g] = grouped
+
+        def quantise_and_multiply(g):
+            codes = work.tile([P, TOKENS], U32, name="codes", align_bytes=64)
+            x_scales = work.tile([P, TOKENS], U8, name="x_scales", align_bytes=64)
+            nc.vector.quantize_mx(
+                out=codes[:].bitcast(FP8X4),
+                scales=x_scales[:],
+                in_=grouped_tiles[g][:].rearrange("p n t -> p (n t)"),
+            )
+            first_row = 4 * (g % PLANES)
+            for b in range(SEQS):
+                nc.tensor.matmul_mx(
+                    out=acc[b][:],
+                    lhsT=codes[:, P * b : P * (b + 1)].bitcast(FP8X4),
+                    lhsT_scale=x_scales[:, P * b : P * (b + 1)],
+                    rhs=w_tiles[g][:].bitcast(FP8X4),
+                    rhs_scale=w_planes[first_row:P, g // PLANES, :],
+                    start=(g == 0),
+                    stop=(g == GROUPS - 1),
+                )
+
+        transpose_group(0)
+        for step in range(GROUPS + 2):
+            if step + LOAD_AHEAD < GROUPS:
+                load_group(step + LOAD_AHEAD)
+            if step + 1 < GROUPS:
+                transpose_group(step + 1)
+            if step < GROUPS:
+                shift_and_mix(step)
+            if 1 <= step <= GROUPS:
+                regroup(step - 1)
+            if step >= 2:
+                quantise_and_multiply(step - 2)
+
+        kept = const.tile([P, SEQS, CO], F32, name="kept")
+        result = const.tile([P, SEQS, CO], F32, name="result")
+        for b in range(SEQS):
+            nc.vector.tensor_tensor(
+                out=kept[:, b, :], in0=acc[b][:], in1=keep_v[:, b, :], op=ALU.mult
+            )
+        for b in range(SEQS):
+            nc.vector.tensor_tensor(
+                out=result[:, b, :], in0=kept[:, b, :], in1=first_part[:, b, :], op=ALU.add
+            )
+            nc.sync.dma_start(out=out[b], in_=result[:, b, :])

@@ -33,6 +33,9 @@ W_BUFS = LOAD_AHEAD + 4
 CARRY_TILES = 2 * PACK
 RUN = 4
 SCALAR_TOKENS = 256
+PARTS = 2
+PART_SEQS = SEQS // PARTS
+PART_TOKENS = PART_SEQS * P
 
 FLOPS = 2 * TOKENS * CHANNELS * CO + 2 * TOKENS * DV * CO
 
@@ -147,45 +150,38 @@ def tile_full_tmix_params_pb_k_kernel(
         mixed_tiles = {}
         grouped_tiles = {}
 
-        def transpose_group(g):
+        def transpose_words(g, u):
             words = x_tiles[g][:].bitcast(F32)
-            for u in range(HALVES):
-                bank = psum_t.tile([P, TOKENS], F32, name="bank", tag="bank")
-                for b in range(SEQS):
-                    nc.tensor.transpose(
-                        bank[:, P * b : P * (b + 1)], words[:, b, u:WORDS:HALVES], ident_f[:]
-                    )
-                banks[g, u] = bank
-
-        def shift_and_mix(g):
-            mixed = work.tile([P, PACK, TOKENS], BF16, name="mixed")
-            for u in range(HALVES):
-                by_seq = banks[g, u][:].bitcast(BF16).rearrange(
-                    "p (b n e) -> p b n e", b=SEQS, e=2
+            bank = psum_t.tile([P, TOKENS], F32, name="bank", tag="bank")
+            for b in range(SEQS):
+                nc.tensor.transpose(
+                    bank[:, P * b : P * (b + 1)], words[:, b, u:WORDS:HALVES], ident_f[:]
                 )
-                for e in range(2):
-                    t = HALVES * u + e
-                    nc.scalar.activation(
-                        out=carry_tiles[(PACK * g + t) % CARRY_TILES][:, :, 1:P],
-                        in_=by_seq[:, :, 0 : P - 1, e],
-                        func=ACT.Copy,
-                        scale=mix_k[:, g, t : t + 1],
-                    )
-            for u in range(HALVES):
-                flat = banks[g, u][:].bitcast(BF16).rearrange("p (n e) -> p n e", e=2)
-                for e in (1, 0):
-                    t = HALVES * u + e
-                    nc.vector.scalar_tensor_tensor(
-                        out=mixed[:, t, :],
-                        in0=flat[:, :, e],
-                        scalar=keep_k[:, g, t : t + 1],
-                        in1=carry_tiles[(PACK * g + t) % CARRY_TILES][:].rearrange(
-                            "p b n -> p (b n)"
-                        ),
-                        op0=ALU.mult,
-                        op1=ALU.add,
-                    )
-            mixed_tiles[g] = mixed
+            banks[g, u] = bank
+
+        def shift_and_mix(g, u):
+            if u == 0:
+                mixed_tiles[g] = work.tile([P, PACK, TOKENS], BF16, name="mixed")
+            by_seq = banks[g, u][:].bitcast(BF16).rearrange("p (b n e) -> p b n e", b=SEQS, e=2)
+            for e in range(2):
+                t = HALVES * u + e
+                nc.scalar.activation(
+                    out=carry_tiles[(PACK * g + t) % CARRY_TILES][:, :, 1:P],
+                    in_=by_seq[:, :, 0 : P - 1, e],
+                    func=ACT.Copy,
+                    scale=mix_k[:, g, t : t + 1],
+                )
+            flat = banks[g, u][:].bitcast(BF16).rearrange("p (n e) -> p n e", e=2)
+            for e in (1, 0):
+                t = HALVES * u + e
+                nc.vector.scalar_tensor_tensor(
+                    out=mixed_tiles[g][:, t, :],
+                    in0=flat[:, :, e],
+                    scalar=keep_k[:, g, t : t + 1],
+                    in1=carry_tiles[(PACK * g + t) % CARRY_TILES][:].rearrange("p b n -> p (b n)"),
+                    op0=ALU.mult,
+                    op1=ALU.add,
+                )
 
         def regroup(g):
             grouped = work.tile([P, TOKENS, PACK], BF16, name="grouped", align_bytes=64)
@@ -196,38 +192,41 @@ def tile_full_tmix_params_pb_k_kernel(
             nc.vector.tensor_copy(out=dst[:, cut:], in_=src[:, cut:])
             grouped_tiles[g] = grouped
 
-        def quantise_and_multiply(g):
-            codes = work.tile([P, TOKENS], U32, name="codes", align_bytes=64)
-            x_scales = work.tile([P, TOKENS], U8, name="x_scales", align_bytes=64)
+        def quantise_and_multiply(g, part):
+            codes = work.tile([P, PART_TOKENS], U32, name="codes", align_bytes=64)
+            x_scales = work.tile([P, PART_TOKENS], U8, name="x_scales", align_bytes=64)
+            tokens = slice(PART_TOKENS * part, PART_TOKENS * (part + 1))
             nc.vector.quantize_mx(
                 out=codes[:].bitcast(FP8X4),
                 scales=x_scales[:],
-                in_=grouped_tiles[g][:].rearrange("p n t -> p (n t)"),
+                in_=grouped_tiles[g][:, tokens, :].rearrange("p n t -> p (n t)"),
             )
             first_row = 4 * (g % PLANES)
-            for b in range(SEQS):
+            for i in range(PART_SEQS):
                 nc.tensor.matmul_mx(
-                    out=acc[b][:],
-                    lhsT=codes[:, P * b : P * (b + 1)].bitcast(FP8X4),
-                    lhsT_scale=x_scales[:, P * b : P * (b + 1)],
+                    out=acc[PART_SEQS * part + i][:],
+                    lhsT=codes[:, P * i : P * (i + 1)].bitcast(FP8X4),
+                    lhsT_scale=x_scales[:, P * i : P * (i + 1)],
                     rhs=w_tiles[g][:].bitcast(FP8X4),
                     rhs_scale=w_planes[first_row:P, g // PLANES, :],
                     start=(g == 0),
                     stop=(g == GROUPS - 1),
                 )
 
-        transpose_group(0)
+        for u in range(HALVES):
+            transpose_words(0, u)
         for step in range(GROUPS + 2):
             if step + LOAD_AHEAD < GROUPS:
                 load_group(step + LOAD_AHEAD)
-            if step + 1 < GROUPS:
-                transpose_group(step + 1)
-            if step < GROUPS:
-                shift_and_mix(step)
+            for part in range(PARTS):
+                if step + 1 < GROUPS:
+                    transpose_words(step + 1, part)
+                if step < GROUPS:
+                    shift_and_mix(step, part)
+                if step >= 2:
+                    quantise_and_multiply(step - 2, part)
             if 1 <= step <= GROUPS:
                 regroup(step - 1)
-            if step >= 2:
-                quantise_and_multiply(step - 2)
 
         kept = const.tile([P, SEQS, CO], F32, name="kept")
         result = const.tile([P, SEQS, CO], F32, name="result")

@@ -28,11 +28,11 @@ PLANES = 4
 QUADRANTS = 4
 
 LOAD_AHEAD = 6
-X_BUFS = LOAD_AHEAD + 2
+X_BUFS = LOAD_AHEAD
 W_BUFS = LOAD_AHEAD + 4
 CARRY_TILES = 2 * PACK
 RUN = 4
-SCALAR_TOKENS = 256
+SCALAR_TOKENS = 160
 PARTS = 2
 PART_SEQS = SEQS // PARTS
 PART_TOKENS = PART_SEQS * P
@@ -49,6 +49,7 @@ def tile_full_tmix_params_pb_k_kernel(
         x_pool = ctx.enter_context(tc.tile_pool(name="x_pool", bufs=X_BUFS))
         w_pool = ctx.enter_context(tc.tile_pool(name="w_pool", bufs=W_BUFS))
         work = ctx.enter_context(tc.tile_pool(name="work", bufs=3))
+        turn = ctx.enter_context(tc.tile_pool(name="turn", bufs=1))
         psum_t = ctx.enter_context(tc.psum_pool(name="psum_t", bufs=4))
         psum_acc = ctx.enter_context(tc.psum_pool(name="psum_acc", bufs=1))
         ctx.enter_context(tc.manual_schedule())
@@ -135,11 +136,11 @@ def tile_full_tmix_params_pb_k_kernel(
             nc.tensor.matmul(out=z[:], lhsT=vhT[:, b, :], rhs=v2_sb[:], start=True, stop=False)
             nc.tensor.matmul(out=z[:], lhsT=ones[:], rhs=bias_rows[:], start=False, stop=True)
             nc.scalar.activation(out=gate[:, b, :], in_=z[:], func=ACT.Sigmoid)
-            nc.gpsimd.tensor_scalar(
+            nc.vector.tensor_scalar(
                 out=keep_v[:, b, :], in0=gate[:, b, :],
                 scalar1=-1.0, scalar2=1.0, op0=ALU.mult, op1=ALU.add,
             )
-            nc.gpsimd.tensor_tensor(
+            nc.vector.tensor_tensor(
                 out=first_part[:, b, :], in0=vf[:, b, :], in1=gate[:, b, :], op=ALU.mult
             )
         acc = [
@@ -149,6 +150,7 @@ def tile_full_tmix_params_pb_k_kernel(
         banks = {}
         mixed_tiles = {}
         grouped_tiles = {}
+        quantised = {}
 
         def transpose_words(g, u):
             words = x_tiles[g][:].bitcast(F32)
@@ -159,9 +161,7 @@ def tile_full_tmix_params_pb_k_kernel(
                 )
             banks[g, u] = bank
 
-        def shift_and_mix(g, u):
-            if u == 0:
-                mixed_tiles[g] = work.tile([P, PACK, TOKENS], BF16, name="mixed")
+        def carry(g, u):
             by_seq = banks[g, u][:].bitcast(BF16).rearrange("p (b n e) -> p b n e", b=SEQS, e=2)
             for e in range(2):
                 t = HALVES * u + e
@@ -171,6 +171,10 @@ def tile_full_tmix_params_pb_k_kernel(
                     func=ACT.Copy,
                     scale=mix_k[:, g, t : t + 1],
                 )
+
+        def mix(g, u):
+            if u == 0:
+                mixed_tiles[g] = work.tile([P, PACK, TOKENS], BF16, name="mixed")
             flat = banks[g, u][:].bitcast(BF16).rearrange("p (n e) -> p n e", e=2)
             for e in (1, 0):
                 t = HALVES * u + e
@@ -184,15 +188,20 @@ def tile_full_tmix_params_pb_k_kernel(
                 )
 
         def regroup(g):
-            grouped = work.tile([P, TOKENS, PACK], BF16, name="grouped", align_bytes=64)
-            src = mixed_tiles[g][:].rearrange("p t (c i) -> p c t i", i=RUN)
-            dst = grouped[:].rearrange("p (c i) t -> p c t i", i=RUN)
-            cut = SCALAR_TOKENS // RUN
-            nc.scalar.copy(out=dst[:, 0:cut], in_=src[:, 0:cut])
-            nc.vector.tensor_copy(out=dst[:, cut:], in_=src[:, cut:])
+            grouped = turn.tile([P, TOKENS, PACK], BF16, name="grouped", align_bytes=64)
+            mixed = mixed_tiles[g]
+            nc.scalar.copy(
+                out=grouped[:, 0:SCALAR_TOKENS, :].rearrange("p (c i) t -> p c t i", i=RUN),
+                in_=mixed[:, :, 0:SCALAR_TOKENS].rearrange("p t (c i) -> p c t i", i=RUN),
+            )
+            nc.gpsimd.tensor_scalar(
+                out=grouped[:, SCALAR_TOKENS:, :],
+                in0=mixed[:, :, SCALAR_TOKENS:].rearrange("p t n -> p n t"),
+                scalar1=1.0, scalar2=0.0, op0=ALU.mult, op1=ALU.add,
+            )
             grouped_tiles[g] = grouped
 
-        def quantise_and_multiply(g, part):
+        def quantise(g, part):
             codes = work.tile([P, PART_TOKENS], U32, name="codes", align_bytes=64)
             x_scales = work.tile([P, PART_TOKENS], U8, name="x_scales", align_bytes=64)
             tokens = slice(PART_TOKENS * part, PART_TOKENS * (part + 1))
@@ -201,6 +210,10 @@ def tile_full_tmix_params_pb_k_kernel(
                 scales=x_scales[:],
                 in_=grouped_tiles[g][:, tokens, :].rearrange("p n t -> p (n t)"),
             )
+            quantised[g, part] = (codes, x_scales)
+
+        def multiply(g, part):
+            codes, x_scales = quantised[g, part]
             first_row = 4 * (g % PLANES)
             for i in range(PART_SEQS):
                 nc.tensor.matmul_mx(
@@ -213,20 +226,29 @@ def tile_full_tmix_params_pb_k_kernel(
                     stop=(g == GROUPS - 1),
                 )
 
+        for g in range(2):
+            for u in range(HALVES):
+                transpose_words(g, u)
         for u in range(HALVES):
-            transpose_words(0, u)
+            carry(0, u)
         for step in range(GROUPS + 2):
             if step + LOAD_AHEAD < GROUPS:
                 load_group(step + LOAD_AHEAD)
-            for part in range(PARTS):
-                if step + 1 < GROUPS:
-                    transpose_words(step + 1, part)
-                if step < GROUPS:
-                    shift_and_mix(step, part)
-                if step >= 2:
-                    quantise_and_multiply(step - 2, part)
+            if step >= 2:
+                for part in range(PARTS):
+                    quantise(step - 2, part)
             if 1 <= step <= GROUPS:
                 regroup(step - 1)
+            for part in range(PARTS):
+                if step >= 2:
+                    multiply(step - 2, part)
+                if step < GROUPS:
+                    mix(step, part)
+                if step + 2 < GROUPS:
+                    transpose_words(step + 2, part)
+            if step + 1 < GROUPS:
+                for u in range(HALVES):
+                    carry(step + 1, u)
 
         kept = const.tile([P, SEQS, CO], F32, name="kept")
         result = const.tile([P, SEQS, CO], F32, name="result")

@@ -54,8 +54,14 @@ def tile_full_tmix_params_pb_k_kernel(
         psum_acc = ctx.enter_context(tc.psum_pool(name="psum_acc", bufs=1))
         ctx.enter_context(tc.manual_schedule())
 
+        ident_f = const.tile([P, P], F32, name="ident_f")
+        make_identity(nc, ident_f[:])
+        ident_b = const.tile([P, P], BF16, name="ident_b")
+        make_identity(nc, ident_b[:])
+        ones = const.tile([P, P], BF16, name="ones")
+        nc.gpsimd.memset(ones[:], 1.0)
+
         w_planes = const.tile([P, GROUPS // PLANES, CO], U8, name="w_planes", align_bytes=64)
-        nc.vector.memset(w_planes[:].bitcast(I32), 0)
         x_tiles = {}
         w_tiles = {}
 
@@ -81,34 +87,31 @@ def tile_full_tmix_params_pb_k_kernel(
 
         xv_rows = const.tile([P, K_PASS], BF16, name="xv_rows")
         nc.vector.memset(xv_rows[:], 0.0)
+        nc.vector.memset(w_planes[:].bitcast(I32), 0)
         nc.scalar.dma_start(
             out=xv_rows[0:GROUPS, :], in_=x_v.rearrange("a b (g k) -> (a b g) k", k=K_PASS)
         )
-        vh = const.tile([P, SEQS, DV], BF16, name="vh")
-        nc.scalar.dma_start(out=vh[:], in_=v_hid.rearrange("b n d -> n b d"))
-        v2_sb = const.tile([DV, CO], BF16, name="v2_sb")
-        nc.scalar.dma_start(out=v2_sb[:], in_=v2)
-        bias_rows = const.tile([P, CO], BF16, name="bias_rows")
-        nc.gpsimd.memset(bias_rows[:], 0.0)
-        nc.scalar.dma_start(out=bias_rows[0:1, :], in_=v0.rearrange("a b c -> (a b) c"))
         for g in range(LOAD_AHEAD):
             load_group(g)
+        vh = const.tile([P, SEQS, DV], BF16, name="vh")
+        nc.sync.dma_start(out=vh[:], in_=v_hid.rearrange("b n d -> n b d"))
+        v2_sb = const.tile([DV, CO], BF16, name="v2_sb")
+        nc.sync.dma_start(out=v2_sb[:], in_=v2)
+        bias_rows = const.tile([P, CO], BF16, name="bias_rows")
+        nc.gpsimd.memset(bias_rows[:], 0.0)
+        nc.sync.dma_start(out=bias_rows[0:1, :], in_=v0.rearrange("a b c -> (a b) c"))
         vf = const.tile([P, SEQS, CO], BF16, name="vf")
-        nc.scalar.dma_start(out=vf[:], in_=v_first.rearrange("b n c -> n b c"))
+        nc.sync.dma_start(out=vf[:], in_=v_first.rearrange("b n c -> n b c"))
 
-        ident_f = const.tile([P, P], F32, name="ident_f")
-        make_identity(nc, ident_f[:])
-        ident_b = const.tile([P, P], BF16, name="ident_b")
-        make_identity(nc, ident_b[:])
-        ones = const.tile([P, P], BF16, name="ones")
-        nc.gpsimd.memset(ones[:], 1.0)
+        table_warmer = const.tile([P, 1], F32, name="table_warmer")
+        nc.scalar.activation(out=table_warmer[:], in_=ident_f[:, 0:1], func=ACT.Sigmoid)
         carry_tiles = []
         for i in range(CARRY_TILES):
             carried = const.tile([P, SEQS, P], F32, name="carried%d" % i)
             nc.vector.memset(carried[:], 0.0)
             carry_tiles.append(carried)
 
-        xv_ps = psum_t.tile([P, HALVES, P], F32, name="xv_ps", tag="bank")
+        xv_ps = psum_acc.tile([P, HALVES, P], F32, name="xv_ps", tag="acc0")
         for u in range(HALVES):
             nc.tensor.transpose(
                 xv_ps[:, u, :], xv_rows[:].bitcast(F32)[:, u:WORDS:HALVES], ident_f[:]
@@ -123,34 +126,43 @@ def tile_full_tmix_params_pb_k_kernel(
             out=keep_k[:], in0=mix_k[:], scalar1=-1.0, scalar2=1.0, op0=ALU.mult, op1=ALU.add
         )
 
-        vhT_ps = psum_t.tile([P, SEQS, P], BF16, name="vhT_ps", tag="bank")
-        for b in range(SEQS):
-            nc.tensor.transpose(vhT_ps[:, b, :], vh[:, b, :], ident_b[:])
+        gate_sums = {}
         vhT = const.tile([DV, SEQS, P], BF16, name="vhT")
-        nc.vector.tensor_copy(out=vhT[:], in_=vhT_ps[:])
         gate = const.tile([P, SEQS, CO], F32, name="gate")
         keep_v = const.tile([P, SEQS, CO], F32, name="keep_v")
         first_part = const.tile([P, SEQS, CO], F32, name="first_part")
-        for b in range(SEQS):
-            z = psum_acc.tile([P, CO], F32, name="z%d" % b, tag="acc%d" % b)
+
+        def turn_v_hid():
+            vhT_ps = psum_t.tile([P, SEQS, P], BF16, name="vhT_ps", tag="bank")
+            for b in range(SEQS):
+                nc.tensor.transpose(vhT_ps[:, b, :], vh[:, b, :], ident_b[:])
+            nc.vector.tensor_copy(out=vhT[:], in_=vhT_ps[:])
+
+        def gate_product(b):
+            z = psum_t.tile([P, CO], F32, name="z", tag="bank")
             nc.tensor.matmul(out=z[:], lhsT=vhT[:, b, :], rhs=v2_sb[:], start=True, stop=False)
             nc.tensor.matmul(out=z[:], lhsT=ones[:], rhs=bias_rows[:], start=False, stop=True)
-            nc.scalar.activation(out=gate[:, b, :], in_=z[:], func=ACT.Sigmoid)
-            nc.vector.tensor_scalar(
-                out=keep_v[:, b, :], in0=gate[:, b, :],
-                scalar1=-1.0, scalar2=1.0, op0=ALU.mult, op1=ALU.add,
-            )
-            nc.vector.tensor_tensor(
-                out=first_part[:, b, :], in0=vf[:, b, :], in1=gate[:, b, :], op=ALU.mult
-            )
-        acc = [
-            psum_acc.tile([P, CO], F32, name="acc%d" % b, tag="acc%d" % b) for b in range(SEQS)
-        ]
+            gate_sums[b] = z
+
+        def gate_sigmoids(seqs):
+            for b in seqs:
+                nc.scalar.activation(out=gate[:, b, :], in_=gate_sums[b][:], func=ACT.Sigmoid)
+            for b in seqs:
+                nc.scalar.activation(
+                    out=keep_v[:, b, :], in_=gate_sums[b][:], func=ACT.Sigmoid, scale=-1.0
+                )
+
+        def first_parts():
+            for b in range(SEQS):
+                nc.vector.tensor_tensor(
+                    out=first_part[:, b, :], in0=vf[:, b, :], in1=gate[:, b, :], op=ALU.mult
+                )
 
         banks = {}
         mixed_tiles = {}
         grouped_tiles = {}
         quantised = {}
+        acc = []
 
         def transpose_words(g, u):
             words = x_tiles[g][:].bitcast(F32)
@@ -231,6 +243,8 @@ def tile_full_tmix_params_pb_k_kernel(
                 transpose_words(g, u)
         for u in range(HALVES):
             carry(0, u)
+        for b in range(SEQS):
+            acc.append(psum_acc.tile([P, CO], F32, name="acc%d" % b, tag="acc%d" % b))
         for step in range(GROUPS + 2):
             if step + LOAD_AHEAD < GROUPS:
                 load_group(step + LOAD_AHEAD)
@@ -246,9 +260,18 @@ def tile_full_tmix_params_pb_k_kernel(
                     mix(step, part)
                 if step + 2 < GROUPS:
                     transpose_words(step + 2, part)
+                elif step < GROUPS:
+                    if step + 2 == GROUPS and part == 0:
+                        turn_v_hid()
+                    gate_product(PARTS * (step + 2 - GROUPS) + part)
             if step + 1 < GROUPS:
                 for u in range(HALVES):
                     carry(step + 1, u)
+            elif step <= GROUPS:
+                first_seq = PART_SEQS * (step + 1 - GROUPS)
+                gate_sigmoids(range(first_seq, first_seq + PART_SEQS))
+            if step == GROUPS:
+                first_parts()
 
         kept = const.tile([P, SEQS, CO], F32, name="kept")
         result = const.tile([P, SEQS, CO], F32, name="result")

@@ -65,13 +65,15 @@ def tile_full_tmix_params_pb_k_kernel(
         x_tiles = {}
         w_tiles = {}
 
-        def load_group(g):
+        def load_x(g):
             x_g = x_pool.tile([P, SEQS, K_PASS], BF16, name="x_g")
             nc.sync.dma_start(
                 out=x_g[:],
                 in_=x[:, :, K_PASS * g : K_PASS * (g + 1)].rearrange("b n k -> n b k"),
             )
             x_tiles[g] = x_g
+
+        def load_w(g):
             if g % PLANES == 0:
                 for q in range(QUADRANTS):
                     nc.sync.dma_start(
@@ -86,13 +88,19 @@ def tile_full_tmix_params_pb_k_kernel(
             w_tiles[g] = w_g
 
         xv_rows = const.tile([P, K_PASS], BF16, name="xv_rows")
-        nc.vector.memset(xv_rows[:], 0.0)
+        for first, last in ((GROUPS, 2 * GROUPS), (2 * GROUPS, P)):
+            nc.vector.memset(xv_rows[first:last, :], 0.0)
         nc.vector.memset(w_planes[:].bitcast(I32), 0)
         nc.scalar.dma_start(
             out=xv_rows[0:GROUPS, :], in_=x_v.rearrange("a b (g k) -> (a b g) k", k=K_PASS)
         )
-        for g in range(LOAD_AHEAD):
-            load_group(g)
+        load_x(0)
+        load_x(1)
+        load_w(0)
+        load_w(1)
+        for g in range(2, LOAD_AHEAD):
+            load_x(g)
+            load_w(g)
         vh = const.tile([P, SEQS, DV], BF16, name="vh")
         nc.sync.dma_start(out=vh[:], in_=v_hid.rearrange("b n d -> n b d"))
         v2_sb = const.tile([DV, CO], BF16, name="v2_sb")
@@ -105,11 +113,8 @@ def tile_full_tmix_params_pb_k_kernel(
 
         table_warmer = const.tile([P, 1], F32, name="table_warmer")
         nc.scalar.activation(out=table_warmer[:], in_=ident_f[:, 0:1], func=ACT.Sigmoid)
-        carry_tiles = []
-        for i in range(CARRY_TILES):
-            carried = const.tile([P, SEQS, P], F32, name="carried%d" % i)
-            nc.vector.memset(carried[:], 0.0)
-            carry_tiles.append(carried)
+        carried = const.tile([P, CARRY_TILES, SEQS, P], F32, name="carried")
+        nc.vector.memset(carried[:, :, :, 0:1], 0.0)
 
         xv_ps = psum_acc.tile([P, HALVES, P], F32, name="xv_ps", tag="acc0")
         for u in range(HALVES):
@@ -178,10 +183,22 @@ def tile_full_tmix_params_pb_k_kernel(
             for e in range(2):
                 t = HALVES * u + e
                 nc.scalar.activation(
-                    out=carry_tiles[(PACK * g + t) % CARRY_TILES][:, :, 1:P],
+                    out=carried[:, (PACK * g + t) % CARRY_TILES, :, 1:P],
                     in_=by_seq[:, :, 0 : P - 1, e],
                     func=ACT.Copy,
                     scale=mix_k[:, g, t : t + 1],
+                )
+
+        def carry_on_vector(g, u):
+            by_seq = banks[g, u][:].bitcast(BF16).rearrange("p (b n e) -> p b n e", b=SEQS, e=2)
+            for e in range(2):
+                t = HALVES * u + e
+                nc.vector.tensor_scalar(
+                    out=carried[:, (PACK * g + t) % CARRY_TILES, :, 1:P],
+                    in0=by_seq[:, :, 0 : P - 1, e],
+                    scalar1=mix_k[:, g, t : t + 1],
+                    scalar2=None,
+                    op0=ALU.mult,
                 )
 
         def mix(g, u):
@@ -194,7 +211,7 @@ def tile_full_tmix_params_pb_k_kernel(
                     out=mixed_tiles[g][:, t, :],
                     in0=flat[:, :, e],
                     scalar=keep_k[:, g, t : t + 1],
-                    in1=carry_tiles[(PACK * g + t) % CARRY_TILES][:].rearrange("p b n -> p (b n)"),
+                    in1=carried[:, (PACK * g + t) % CARRY_TILES, :, :].rearrange("p b n -> p (b n)"),
                     op0=ALU.mult,
                     op1=ALU.add,
                 )
@@ -241,13 +258,14 @@ def tile_full_tmix_params_pb_k_kernel(
         for g in range(2):
             for u in range(HALVES):
                 transpose_words(g, u)
-        for u in range(HALVES):
-            carry(0, u)
+        carry(0, 0)
+        carry_on_vector(0, 1)
         for b in range(SEQS):
             acc.append(psum_acc.tile([P, CO], F32, name="acc%d" % b, tag="acc%d" % b))
         for step in range(GROUPS + 2):
             if step + LOAD_AHEAD < GROUPS:
-                load_group(step + LOAD_AHEAD)
+                load_x(step + LOAD_AHEAD)
+                load_w(step + LOAD_AHEAD)
             if step >= 2:
                 for part in range(PARTS):
                     quantise(step - 2, part)

@@ -32,7 +32,7 @@ X_BUFS = LOAD_AHEAD
 W_BUFS = LOAD_AHEAD + 4
 CARRY_TILES = 2 * PACK
 RUN = 4
-SCALAR_TOKENS = 160
+SCALAR_TOKENS = 176
 PARTS = 2
 PART_SEQS = SEQS // PARTS
 PART_TOKENS = PART_SEQS * P

@@ -32,7 +32,7 @@ X_BUFS = LOAD_AHEAD
 W_BUFS = LOAD_AHEAD + 4
 CARRY_TILES = 2 * PACK
 RUN = 4
-SCALAR_TOKENS = 176
+SCALAR_TOKENS = 152
 PARTS = 2
 PART_SEQS = SEQS // PARTS
 PART_TOKENS = PART_SEQS * P
@@ -49,7 +49,7 @@ def tile_full_tmix_params_pb_k_kernel(
         x_pool = ctx.enter_context(tc.tile_pool(name="x_pool", bufs=X_BUFS))
         w_pool = ctx.enter_context(tc.tile_pool(name="w_pool", bufs=W_BUFS))
         work = ctx.enter_context(tc.tile_pool(name="work", bufs=3))
-        turn = ctx.enter_context(tc.tile_pool(name="turn", bufs=1))
+        turn = ctx.enter_context(tc.tile_pool(name="turn", bufs=2))
         psum_t = ctx.enter_context(tc.psum_pool(name="psum_t", bufs=4))
         psum_acc = ctx.enter_context(tc.psum_pool(name="psum_acc", bufs=1))
         ctx.enter_context(tc.manual_schedule())
@@ -230,25 +230,24 @@ def tile_full_tmix_params_pb_k_kernel(
             )
             grouped_tiles[g] = grouped
 
-        def quantise(g, part):
-            codes = work.tile([P, PART_TOKENS], U32, name="codes", align_bytes=64)
-            x_scales = work.tile([P, PART_TOKENS], U8, name="x_scales", align_bytes=64)
-            tokens = slice(PART_TOKENS * part, PART_TOKENS * (part + 1))
+        def quantise(g):
+            codes = work.tile([P, TOKENS], U32, name="codes", align_bytes=64)
+            x_scales = work.tile([P, TOKENS], U8, name="x_scales", align_bytes=64)
             nc.vector.quantize_mx(
                 out=codes[:].bitcast(FP8X4),
                 scales=x_scales[:],
-                in_=grouped_tiles[g][:, tokens, :].rearrange("p n t -> p (n t)"),
+                in_=grouped_tiles[g][:].rearrange("p n t -> p (n t)"),
             )
-            quantised[g, part] = (codes, x_scales)
+            quantised[g] = (codes, x_scales)
 
         def multiply(g, part):
-            codes, x_scales = quantised[g, part]
+            codes, x_scales = quantised[g]
             first_row = 4 * (g % PLANES)
-            for i in range(PART_SEQS):
+            for b in range(PART_SEQS * part, PART_SEQS * (part + 1)):
                 nc.tensor.matmul_mx(
-                    out=acc[PART_SEQS * part + i][:],
-                    lhsT=codes[:, P * i : P * (i + 1)].bitcast(FP8X4),
-                    lhsT_scale=x_scales[:, P * i : P * (i + 1)],
+                    out=acc[b][:],
+                    lhsT=codes[:, P * b : P * (b + 1)].bitcast(FP8X4),
+                    lhsT_scale=x_scales[:, P * b : P * (b + 1)],
                     rhs=w_tiles[g][:].bitcast(FP8X4),
                     rhs_scale=w_planes[first_row:P, g // PLANES, :],
                     start=(g == 0),
@@ -267,8 +266,7 @@ def tile_full_tmix_params_pb_k_kernel(
                 load_x(step + LOAD_AHEAD)
                 load_w(step + LOAD_AHEAD)
             if step >= 2:
-                for part in range(PARTS):
-                    quantise(step - 2, part)
+                quantise(step - 2)
             if 1 <= step <= GROUPS:
                 regroup(step - 1)
             for part in range(PARTS):

@@ -31,6 +31,7 @@ LOAD_AHEAD = 6
 X_BUFS = LOAD_AHEAD
 W_BUFS = LOAD_AHEAD + 4
 CARRY_TILES = 2 * PACK
+LAST_SCALAR_TOKENS = 192
 RUN = 4
 SCALAR_TOKENS = 152
 PARTS = 2
@@ -157,8 +158,8 @@ def tile_full_tmix_params_pb_k_kernel(
                     out=keep_v[:, b, :], in_=gate_sums[b][:], func=ACT.Sigmoid, scale=-1.0
                 )
 
-        def first_parts():
-            for b in range(SEQS):
+        def first_parts(seqs):
+            for b in seqs:
                 nc.vector.tensor_tensor(
                     out=first_part[:, b, :], in0=vf[:, b, :], in1=gate[:, b, :], op=ALU.mult
                 )
@@ -230,6 +231,19 @@ def tile_full_tmix_params_pb_k_kernel(
             )
             grouped_tiles[g] = grouped
 
+        def regroup_last(g):
+            grouped = turn.tile([P, TOKENS, PACK], BF16, name="grouped", align_bytes=64)
+            mixed = mixed_tiles[g]
+            for move, first, last in (
+                (nc.scalar.copy, 0, LAST_SCALAR_TOKENS),
+                (nc.vector.tensor_copy, LAST_SCALAR_TOKENS, TOKENS),
+            ):
+                move(
+                    out=grouped[:, first:last, :].rearrange("p (c i) t -> p c t i", i=RUN),
+                    in_=mixed[:, :, first:last].rearrange("p t (c i) -> p c t i", i=RUN),
+                )
+            grouped_tiles[g] = grouped
+
         def quantise(g):
             codes = work.tile([P, TOKENS], U32, name="codes", align_bytes=64)
             x_scales = work.tile([P, TOKENS], U8, name="x_scales", align_bytes=64)
@@ -267,8 +281,11 @@ def tile_full_tmix_params_pb_k_kernel(
                 load_w(step + LOAD_AHEAD)
             if step >= 2:
                 quantise(step - 2)
-            if 1 <= step <= GROUPS:
+            if 1 <= step < GROUPS:
                 regroup(step - 1)
+            if step == GROUPS:
+                regroup_last(step - 1)
+                first_parts((0, 1))
             for part in range(PARTS):
                 if step >= 2:
                     multiply(step - 2, part)
@@ -286,17 +303,24 @@ def tile_full_tmix_params_pb_k_kernel(
             elif step <= GROUPS:
                 first_seq = PART_SEQS * (step + 1 - GROUPS)
                 gate_sigmoids(range(first_seq, first_seq + PART_SEQS))
-            if step == GROUPS:
-                first_parts()
 
         kept = const.tile([P, SEQS, CO], F32, name="kept")
         result = const.tile([P, SEQS, CO], F32, name="result")
-        for b in range(SEQS):
+
+        def keep(b):
             nc.vector.tensor_tensor(
                 out=kept[:, b, :], in0=acc[b][:], in1=keep_v[:, b, :], op=ALU.mult
             )
-        for b in range(SEQS):
+
+        def finish(b):
             nc.vector.tensor_tensor(
                 out=result[:, b, :], in0=kept[:, b, :], in1=first_part[:, b, :], op=ALU.add
             )
             nc.sync.dma_start(out=out[b], in_=result[:, b, :])
+
+        first_parts((2, 3))
+        keep(0)
+        for b in range(1, SEQS):
+            keep(b)
+            finish(b - 1)
+        finish(SEQS - 1)

@@ -68,10 +68,14 @@ def tile_full_tmix_params_pb_k_kernel(
 
         def load_x(g):
             x_g = x_pool.tile([P, SEQS, K_PASS], BF16, name="x_g")
-            nc.sync.dma_start(
-                out=x_g[:],
-                in_=x[:, :, K_PASS * g : K_PASS * (g + 1)].rearrange("b n k -> n b k"),
-            )
+            size = 1 if g == 0 else SEQS
+            for b in range(0, SEQS, size):
+                nc.sync.dma_start(
+                    out=x_g[:, b : b + size, :],
+                    in_=x[b : b + size, :, K_PASS * g : K_PASS * (g + 1)].rearrange(
+                        "b n k -> n b k"
+                    ),
+                )
             x_tiles[g] = x_g
 
         def load_w(g):
@@ -170,14 +174,20 @@ def tile_full_tmix_params_pb_k_kernel(
         quantised = {}
         acc = []
 
+        def open_bank(g, u):
+            banks[g, u] = psum_t.tile([P, TOKENS], F32, name="bank", tag="bank")
+
+        def transpose_one(g, u, b):
+            nc.tensor.transpose(
+                banks[g, u][:, P * b : P * (b + 1)],
+                x_tiles[g][:].bitcast(F32)[:, b, u:WORDS:HALVES],
+                ident_f[:],
+            )
+
         def transpose_words(g, u):
-            words = x_tiles[g][:].bitcast(F32)
-            bank = psum_t.tile([P, TOKENS], F32, name="bank", tag="bank")
+            open_bank(g, u)
             for b in range(SEQS):
-                nc.tensor.transpose(
-                    bank[:, P * b : P * (b + 1)], words[:, b, u:WORDS:HALVES], ident_f[:]
-                )
-            banks[g, u] = bank
+                transpose_one(g, u, b)
 
         def carry(g, u):
             by_seq = banks[g, u][:].bitcast(BF16).rearrange("p (b n e) -> p b n e", b=SEQS, e=2)
@@ -268,9 +278,13 @@ def tile_full_tmix_params_pb_k_kernel(
                     stop=(g == GROUPS - 1),
                 )
 
-        for g in range(2):
+        for u in range(HALVES):
+            open_bank(0, u)
+        for b in range(SEQS):
             for u in range(HALVES):
-                transpose_words(g, u)
+                transpose_one(0, u, b)
+        for u in range(HALVES):
+            transpose_words(1, u)
         carry(0, 0)
         carry_on_vector(0, 1)
         for b in range(SEQS):
@@ -312,15 +326,15 @@ def tile_full_tmix_params_pb_k_kernel(
                 out=kept[:, b, :], in0=acc[b][:], in1=keep_v[:, b, :], op=ALU.mult
             )
 
-        def finish(b):
-            nc.vector.tensor_tensor(
+        def finish(engine, b):
+            engine.tensor_tensor(
                 out=result[:, b, :], in0=kept[:, b, :], in1=first_part[:, b, :], op=ALU.add
             )
             nc.sync.dma_start(out=out[b], in_=result[:, b, :])
 
         first_parts((2, 3))
-        keep(0)
-        for b in range(1, SEQS):
+        for b in range(SEQS):
             keep(b)
-            finish(b - 1)
-        finish(SEQS - 1)
+        finish(nc.gpsimd, 0)
+        for b in range(1, SEQS):
+            finish(nc.vector, b)

@@ -29,9 +29,10 @@ QUADRANTS = 4
 
 LOAD_AHEAD = 6
 X_BUFS = LOAD_AHEAD
-W_BUFS = LOAD_AHEAD + 4
+W_LAG = 2
+W_BUFS = LOAD_AHEAD + 4 - W_LAG
 CARRY_TILES = 2 * PACK
-LAST_SCALAR_TOKENS = 192
+LAST_SCALAR_TOKENS = 320
 RUN = 4
 SCALAR_TOKENS = 152
 PARTS = 2
@@ -68,7 +69,7 @@ def tile_full_tmix_params_pb_k_kernel(
 
         def load_x(g):
             x_g = x_pool.tile([P, SEQS, K_PASS], BF16, name="x_g")
-            size = 1 if g == 0 else SEQS
+            size = 1 if g < 2 else SEQS
             for b in range(0, SEQS, size):
                 nc.sync.dma_start(
                     out=x_g[:, b : b + size, :],
@@ -92,6 +93,8 @@ def tile_full_tmix_params_pb_k_kernel(
             )
             w_tiles[g] = w_g
 
+        idle_rows = const.tile([P, CO], BF16, name="idle_rows")
+        nc.vector.memset(idle_rows[:], 0.0)
         xv_rows = const.tile([P, K_PASS], BF16, name="xv_rows")
         for first, last in ((GROUPS, 2 * GROUPS), (2 * GROUPS, P)):
             nc.vector.memset(xv_rows[first:last, :], 0.0)
@@ -99,13 +102,10 @@ def tile_full_tmix_params_pb_k_kernel(
         nc.scalar.dma_start(
             out=xv_rows[0:GROUPS, :], in_=x_v.rearrange("a b (g k) -> (a b g) k", k=K_PASS)
         )
-        load_x(0)
-        load_x(1)
-        load_w(0)
-        load_w(1)
-        for g in range(2, LOAD_AHEAD):
+        for g in range(LOAD_AHEAD):
             load_x(g)
-            load_w(g)
+            if g >= W_LAG:
+                load_w(g - W_LAG)
         vh = const.tile([P, SEQS, DV], BF16, name="vh")
         nc.sync.dma_start(out=vh[:], in_=v_hid.rearrange("b n d -> n b d"))
         v2_sb = const.tile([DV, CO], BF16, name="v2_sb")
@@ -121,11 +121,21 @@ def tile_full_tmix_params_pb_k_kernel(
         carried = const.tile([P, CARRY_TILES, SEQS, P], F32, name="carried")
         nc.vector.memset(carried[:, :, :, 0:1], 0.0)
 
+        idle_ps = psum_acc.tile([P, CO], F32, name="idle_ps", tag="acc1")
+
+        def keep_clock(count):
+            for i in range(count):
+                nc.tensor.matmul(
+                    out=idle_ps[:], lhsT=idle_rows[:, 0:P], rhs=idle_rows[:], start=True, stop=True
+                )
+
+        keep_clock(4)
         xv_ps = psum_acc.tile([P, HALVES, P], F32, name="xv_ps", tag="acc0")
         for u in range(HALVES):
             nc.tensor.transpose(
                 xv_ps[:, u, :], xv_rows[:].bitcast(F32)[:, u:WORDS:HALVES], ident_f[:]
             )
+        keep_clock(1)
         mix_k = const.tile([P, GROUPS, PACK], F32, name="mix_k")
         nc.vector.tensor_copy(
             out=mix_k[:].rearrange("p g (u e) -> p u g e", u=HALVES),
@@ -278,23 +288,26 @@ def tile_full_tmix_params_pb_k_kernel(
                     stop=(g == GROUPS - 1),
                 )
 
-        for u in range(HALVES):
-            open_bank(0, u)
-        for b in range(SEQS):
+        for g in range(2):
             for u in range(HALVES):
-                transpose_one(0, u, b)
-        for u in range(HALVES):
-            transpose_words(1, u)
+                open_bank(g, u)
+            for b in range(SEQS):
+                for u in range(HALVES):
+                    transpose_one(g, u, b)
+                if b % PART_SEQS == PART_SEQS - 1:
+                    keep_clock(1)
         carry(0, 0)
         carry_on_vector(0, 1)
-        for b in range(SEQS):
-            acc.append(psum_acc.tile([P, CO], F32, name="acc%d" % b, tag="acc%d" % b))
         for step in range(GROUPS + 2):
             if step + LOAD_AHEAD < GROUPS:
                 load_x(step + LOAD_AHEAD)
-                load_w(step + LOAD_AHEAD)
+            if step + LOAD_AHEAD - W_LAG < GROUPS:
+                load_w(step + LOAD_AHEAD - W_LAG)
             if step >= 2:
                 quantise(step - 2)
+            if step == 2:
+                for b in range(SEQS):
+                    acc.append(psum_acc.tile([P, CO], F32, name="acc%d" % b, tag="acc%d" % b))
             if 1 <= step < GROUPS:
                 regroup(step - 1)
             if step == GROUPS:
@@ -307,6 +320,8 @@ def tile_full_tmix_params_pb_k_kernel(
                     mix(step, part)
                 if step + 2 < GROUPS:
                     transpose_words(step + 2, part)
+                    if step < 2:
+                        keep_clock(1)
                 elif step < GROUPS:
                     if step + 2 == GROUPS and part == 0:
                         turn_v_hid()

@@ -34,7 +34,7 @@ W_BUFS = LOAD_AHEAD + 4 - W_LAG
 CARRY_TILES = 2 * PACK
 LAST_SCALAR_TOKENS = 320
 RUN = 4
-SCALAR_TOKENS = 152
+SCALAR_TOKENS = 128
 PARTS = 2
 PART_SEQS = SEQS // PARTS
 PART_TOKENS = PART_SEQS * P
@@ -245,8 +245,8 @@ def tile_full_tmix_params_pb_k_kernel(
                 in_=mixed[:, :, 0:SCALAR_TOKENS].rearrange("p t (c i) -> p c t i", i=RUN),
             )
             nc.gpsimd.tensor_scalar(
-                out=grouped[:, SCALAR_TOKENS:, :],
-                in0=mixed[:, :, SCALAR_TOKENS:].rearrange("p t n -> p n t"),
+                out=grouped[:, SCALAR_TOKENS:, :].rearrange("p (c i) t -> p c t i", i=RUN),
+                in0=mixed[:, :, SCALAR_TOKENS:].rearrange("p t (c i) -> p c t i", i=RUN),
                 scalar1=1.0, scalar2=0.0, op0=ALU.mult, op1=ALU.add,
             )
             grouped_tiles[g] = grouped
@@ -314,8 +314,11 @@ def tile_full_tmix_params_pb_k_kernel(
                 regroup_last(step - 1)
                 first_parts((0, 1))
             for part in range(PARTS):
-                if step >= 2:
+                if step >= 2 and step % 2 == 0:
                     multiply(step - 2, part)
+                elif step >= 2 and part == 0:
+                    for each in range(PARTS):
+                        multiply(step - 2, each)
                 if step < GROUPS:
                     mix(step, part)
                 if step + 2 < GROUPS:

from contextlib import ExitStack

import concourse.mybir as mybir
from concourse.masks import make_identity

F32 = mybir.dt.float32
BF16 = mybir.dt.bfloat16
U8 = mybir.dt.uint8
U32 = mybir.dt.uint32
I32 = mybir.dt.int32
FP8X4 = mybir.dt.float8_e4m3fn_x4
ACT = mybir.ActivationFunctionType
ALU = mybir.AluOpType

P = 128
SEQS = 4
TOKENS = SEQS * P
CHANNELS = 16384
CO = 512
DV = 128
PACK = 4
K_PASS = P * PACK
GROUPS = CHANNELS // K_PASS
HALVES = 2
WORDS = K_PASS // 2

PLANES = 4
QUADRANTS = 4

LOAD_AHEAD = 6
X_BUFS = LOAD_AHEAD
W_LAG = 2
W_BUFS = LOAD_AHEAD + 4 - W_LAG
CARRY_TILES = 2 * PACK
LAST_SCALAR_TOKENS = 320
RUN = 4
SCALAR_TOKENS = 128
PARTS = 2
PART_SEQS = SEQS // PARTS
PART_TOKENS = PART_SEQS * P

FLOPS = 2 * TOKENS * CHANNELS * CO + 2 * TOKENS * DV * CO


def tile_full_tmix_params_pb_k_kernel(
    tc, x, x_v, W_v_words, W_v_scales, v_hid, v2, v0, v_first, out
):
    nc = tc.nc
    with ExitStack() as ctx:
        const = ctx.enter_context(tc.tile_pool(name="const", bufs=1))
        x_pool = ctx.enter_context(tc.tile_pool(name="x_pool", bufs=X_BUFS))
        w_pool = ctx.enter_context(tc.tile_pool(name="w_pool", bufs=W_BUFS))
        work = ctx.enter_context(tc.tile_pool(name="work", bufs=3))
        turn = ctx.enter_context(tc.tile_pool(name="turn", bufs=2))
        psum_t = ctx.enter_context(tc.psum_pool(name="psum_t", bufs=4))
        psum_acc = ctx.enter_context(tc.psum_pool(name="psum_acc", bufs=1))
        ctx.enter_context(tc.manual_schedule())

        ident_f = const.tile([P, P], F32, name="ident_f")
        make_identity(nc, ident_f[:])
        ident_b = const.tile([P, P], BF16, name="ident_b")
        make_identity(nc, ident_b[:])
        ones = const.tile([P, P], BF16, name="ones")
        nc.gpsimd.memset(ones[:], 1.0)

        w_planes = const.tile([P, GROUPS // PLANES, CO], U8, name="w_planes", align_bytes=64)
        x_tiles = {}
        w_tiles = {}

        def load_x(g):
            x_g = x_pool.tile([P, SEQS, K_PASS], BF16, name="x_g")
            size = 1 if g < 2 else SEQS
            for b in range(0, SEQS, size):
                nc.sync.dma_start(
                    out=x_g[:, b : b + size, :],
                    in_=x[b : b + size, :, K_PASS * g : K_PASS * (g + 1)].rearrange(
                        "b n k -> n b k"
                    ),
                )
            x_tiles[g] = x_g

        def load_w(g):
            if g % PLANES == 0:
                for q in range(QUADRANTS):
                    nc.sync.dma_start(
                        out=w_planes[32 * q : 32 * q + 4 * PLANES, g // PLANES, :].bitcast(I32),
                        in_=W_v_scales[g : g + PLANES, 4 * q : 4 * q + 4, :].bitcast(I32),
                    )
            w_g = w_pool.tile([P, CO], U32, name="w_g", align_bytes=64)
            nc.sync.dma_start(
                out=w_g[:].bitcast(I32),
                in_=W_v_words[g].rearrange("p n t -> p (n t)").bitcast(I32),
            )
            w_tiles[g] = w_g

        idle_rows = const.tile([P, CO], BF16, name="idle_rows")
        nc.vector.memset(idle_rows[:], 0.0)
        xv_rows = const.tile([P, K_PASS], BF16, name="xv_rows")
        for first, last in ((GROUPS, 2 * GROUPS), (2 * GROUPS, P)):
            nc.vector.memset(xv_rows[first:last, :], 0.0)
        nc.vector.memset(w_planes[:].bitcast(I32), 0)
        nc.scalar.dma_start(
            out=xv_rows[0:GROUPS, :], in_=x_v.rearrange("a b (g k) -> (a b g) k", k=K_PASS)
        )
        for g in range(LOAD_AHEAD):
            load_x(g)
            if g >= W_LAG:
                load_w(g - W_LAG)
        vh = const.tile([P, SEQS, DV], BF16, name="vh")
        nc.sync.dma_start(out=vh[:], in_=v_hid.rearrange("b n d -> n b d"))
        v2_sb = const.tile([DV, CO], BF16, name="v2_sb")
        nc.sync.dma_start(out=v2_sb[:], in_=v2)
        bias_rows = const.tile([P, CO], BF16, name="bias_rows")
        nc.gpsimd.memset(bias_rows[:], 0.0)
        nc.sync.dma_start(out=bias_rows[0:1, :], in_=v0.rearrange("a b c -> (a b) c"))
        vf = const.tile([P, SEQS, CO], BF16, name="vf")
        nc.sync.dma_start(out=vf[:], in_=v_first.rearrange("b n c -> n b c"))

        table_warmer = const.tile([P, 1], F32, name="table_warmer")
        nc.scalar.activation(out=table_warmer[:], in_=ident_f[:, 0:1], func=ACT.Sigmoid)
        carried = const.tile([P, CARRY_TILES, SEQS, P], F32, name="carried")
        nc.vector.memset(carried[:, :, :, 0:1], 0.0)

        idle_ps = psum_acc.tile([P, CO], F32, name="idle_ps", tag="acc1")

        def keep_clock(count):
            for i in range(count):
                nc.tensor.matmul(
                    out=idle_ps[:], lhsT=idle_rows[:, 0:P], rhs=idle_rows[:], start=True, stop=True
                )

        keep_clock(4)
        xv_ps = psum_acc.tile([P, HALVES, P], F32, name="xv_ps", tag="acc0")
        for u in range(HALVES):
            nc.tensor.transpose(
                xv_ps[:, u, :], xv_rows[:].bitcast(F32)[:, u:WORDS:HALVES], ident_f[:]
            )
        keep_clock(1)
        mix_k = const.tile([P, GROUPS, PACK], F32, name="mix_k")
        nc.vector.tensor_copy(
            out=mix_k[:].rearrange("p g (u e) -> p u g e", u=HALVES),
            in_=xv_ps[:].bitcast(BF16).rearrange("p u (g e) -> p u g e", e=2)[:, :, 0:GROUPS, :],
        )
        keep_k = const.tile([P, GROUPS, PACK], F32, name="keep_k")
        nc.vector.tensor_scalar(
            out=keep_k[:], in0=mix_k[:], scalar1=-1.0, scalar2=1.0, op0=ALU.mult, op1=ALU.add
        )

        gate_sums = {}
        vhT = const.tile([DV, SEQS, P], BF16, name="vhT")
        gate = const.tile([P, SEQS, CO], F32, name="gate")
        keep_v = const.tile([P, SEQS, CO], F32, name="keep_v")
        first_part = const.tile([P, SEQS, CO], F32, name="first_part")

        def turn_v_hid():
            vhT_ps = psum_t.tile([P, SEQS, P], BF16, name="vhT_ps", tag="bank")
            for b in range(SEQS):
                nc.tensor.transpose(vhT_ps[:, b, :], vh[:, b, :], ident_b[:])
            nc.vector.tensor_copy(out=vhT[:], in_=vhT_ps[:])

        def gate_product(b):
            z = psum_t.tile([P, CO], F32, name="z", tag="bank")
            nc.tensor.matmul(out=z[:], lhsT=vhT[:, b, :], rhs=v2_sb[:], start=True, stop=False)
            nc.tensor.matmul(out=z[:], lhsT=ones[:], rhs=bias_rows[:], start=False, stop=True)
            gate_sums[b] = z

        def gate_sigmoids(seqs):
            for b in seqs:
                nc.scalar.activation(out=gate[:, b, :], in_=gate_sums[b][:], func=ACT.Sigmoid)
            for b in seqs:
                nc.scalar.activation(
                    out=keep_v[:, b, :], in_=gate_sums[b][:], func=ACT.Sigmoid, scale=-1.0
                )

        def first_parts(seqs):
            for b in seqs:
                nc.vector.tensor_tensor(
                    out=first_part[:, b, :], in0=vf[:, b, :], in1=gate[:, b, :], op=ALU.mult
                )

        banks = {}
        mixed_tiles = {}
        grouped_tiles = {}
        quantised = {}
        acc = []

        def open_bank(g, u):
            banks[g, u] = psum_t.tile([P, TOKENS], F32, name="bank", tag="bank")

        def transpose_one(g, u, b):
            nc.tensor.transpose(
                banks[g, u][:, P * b : P * (b + 1)],
                x_tiles[g][:].bitcast(F32)[:, b, u:WORDS:HALVES],
                ident_f[:],
            )

        def transpose_words(g, u):
            open_bank(g, u)
            for b in range(SEQS):
                transpose_one(g, u, b)

        def carry(g, u):
            by_seq = banks[g, u][:].bitcast(BF16).rearrange("p (b n e) -> p b n e", b=SEQS, e=2)
            for e in range(2):
                t = HALVES * u + e
                nc.scalar.activation(
                    out=carried[:, (PACK * g + t) % CARRY_TILES, :, 1:P],
                    in_=by_seq[:, :, 0 : P - 1, e],
                    func=ACT.Copy,
                    scale=mix_k[:, g, t : t + 1],
                )

        def carry_on_vector(g, u):
            by_seq = banks[g, u][:].bitcast(BF16).rearrange("p (b n e) -> p b n e", b=SEQS, e=2)
            for e in range(2):
                t = HALVES * u + e
                nc.vector.tensor_scalar(
                    out=carried[:, (PACK * g + t) % CARRY_TILES, :, 1:P],
                    in0=by_seq[:, :, 0 : P - 1, e],
                    scalar1=mix_k[:, g, t : t + 1],
                    scalar2=None,
                    op0=ALU.mult,
                )

        def mix(g, u):
            if u == 0:
                mixed_tiles[g] = work.tile([P, PACK, TOKENS], BF16, name="mixed")
            flat = banks[g, u][:].bitcast(BF16).rearrange("p (n e) -> p n e", e=2)
            for e in (1, 0):
                t = HALVES * u + e
                nc.vector.scalar_tensor_tensor(
                    out=mixed_tiles[g][:, t, :],
                    in0=flat[:, :, e],
                    scalar=keep_k[:, g, t : t + 1],
                    in1=carried[:, (PACK * g + t) % CARRY_TILES, :, :].rearrange("p b n -> p (b n)"),
                    op0=ALU.mult,
                    op1=ALU.add,
                )

        def regroup(g):
            grouped = turn.tile([P, TOKENS, PACK], BF16, name="grouped", align_bytes=64)
            mixed = mixed_tiles[g]
            nc.scalar.copy(
                out=grouped[:, 0:SCALAR_TOKENS, :].rearrange("p (c i) t -> p c t i", i=RUN),
                in_=mixed[:, :, 0:SCALAR_TOKENS].rearrange("p t (c i) -> p c t i", i=RUN),
            )
            nc.gpsimd.tensor_scalar(
                out=grouped[:, SCALAR_TOKENS:, :].rearrange("p (c i) t -> p c t i", i=RUN),
                in0=mixed[:, :, SCALAR_TOKENS:].rearrange("p t (c i) -> p c t i", i=RUN),
                scalar1=1.0, scalar2=0.0, op0=ALU.mult, op1=ALU.add,
            )
            grouped_tiles[g] = grouped

        def regroup_last(g):
            grouped = turn.tile([P, TOKENS, PACK], BF16, name="grouped", align_bytes=64)
            mixed = mixed_tiles[g]
            for move, first, last in (
                (nc.scalar.copy, 0, LAST_SCALAR_TOKENS),
                (nc.vector.tensor_copy, LAST_SCALAR_TOKENS, TOKENS),
            ):
                move(
                    out=grouped[:, first:last, :].rearrange("p (c i) t -> p c t i", i=RUN),
                    in_=mixed[:, :, first:last].rearrange("p t (c i) -> p c t i", i=RUN),
                )
            grouped_tiles[g] = grouped

        def quantise(g):
            codes = work.tile([P, TOKENS], U32, name="codes", align_bytes=64)
            x_scales = work.tile([P, TOKENS], U8, name="x_scales", align_bytes=64)
            nc.vector.quantize_mx(
                out=codes[:].bitcast(FP8X4),
                scales=x_scales[:],
                in_=grouped_tiles[g][:].rearrange("p n t -> p (n t)"),
            )
            quantised[g] = (codes, x_scales)

        def multiply(g, part):
            codes, x_scales = quantised[g]
            first_row = 4 * (g % PLANES)
            for b in range(PART_SEQS * part, PART_SEQS * (part + 1)):
                nc.tensor.matmul_mx(
                    out=acc[b][:],
                    lhsT=codes[:, P * b : P * (b + 1)].bitcast(FP8X4),
                    lhsT_scale=x_scales[:, P * b : P * (b + 1)],
                    rhs=w_tiles[g][:].bitcast(FP8X4),
                    rhs_scale=w_planes[first_row:P, g // PLANES, :],
                    start=(g == 0),
                    stop=(g == GROUPS - 1),
                )

        for g in range(2):
            for u in range(HALVES):
                open_bank(g, u)
            for b in range(SEQS):
                for u in range(HALVES):
                    transpose_one(g, u, b)
                if b % PART_SEQS == PART_SEQS - 1:
                    keep_clock(1)
        carry(0, 0)
        carry_on_vector(0, 1)
        for step in range(GROUPS + 2):
            if step + LOAD_AHEAD < GROUPS:
                load_x(step + LOAD_AHEAD)
            if step + LOAD_AHEAD - W_LAG < GROUPS:
                load_w(step + LOAD_AHEAD - W_LAG)
            if step >= 2:
                quantise(step - 2)
            if step == 2:
                for b in range(SEQS):
                    acc.append(psum_acc.tile([P, CO], F32, name="acc%d" % b, tag="acc%d" % b))
            if 1 <= step < GROUPS:
                regroup(step - 1)
            if step == GROUPS:
                regroup_last(step - 1)
                first_parts((0, 1))
            for part in range(PARTS):
                if step >= 2 and step % 2 == 0:
                    multiply(step - 2, part)
                elif step >= 2 and part == 0:
                    for each in range(PARTS):
                        multiply(step - 2, each)
                if step < GROUPS:
                    mix(step, part)
                if step + 2 < GROUPS:
                    transpose_words(step + 2, part)
                    if step < 2:
                        keep_clock(1)
                elif step < GROUPS:
                    if step + 2 == GROUPS and part == 0:
                        turn_v_hid()
                    gate_product(PARTS * (step + 2 - GROUPS) + part)
            if step + 1 < GROUPS:
                for u in range(HALVES):
                    carry(step + 1, u)
            elif step <= GROUPS:
                first_seq = PART_SEQS * (step + 1 - GROUPS)
                gate_sigmoids(range(first_seq, first_seq + PART_SEQS))

        kept = const.tile([P, SEQS, CO], F32, name="kept")
        result = const.tile([P, SEQS, CO], F32, name="result")

        def keep(b):
            nc.vector.tensor_tensor(
                out=kept[:, b, :], in0=acc[b][:], in1=keep_v[:, b, :], op=ALU.mult
            )

        def finish(engine, b):
            engine.tensor_tensor(
                out=result[:, b, :], in0=kept[:, b, :], in1=first_part[:, b, :], op=ALU.add
            )
            nc.sync.dma_start(out=out[b], in_=result[:, b, :])

        first_parts((2, 3))
        for b in range(SEQS):
            keep(b)
        finish(nc.gpsimd, 0)
        for b in range(1, SEQS):
            finish(nc.vector, b)
